import numpy as np
import ml_dtypes


def mxq(x, axis, fmt="e4m3"):
    dtype, down = {"e4m3": (ml_dtypes.float8_e4m3fn, 7), "e5m2": (ml_dtypes.float8_e5m2, 14)}[fmt]
    v = np.moveaxis(np.asarray(x, np.float32).astype(ml_dtypes.bfloat16).astype(np.float64), axis, -1)
    blocks = v.reshape(v.shape[:-1] + (-1, 32))
    amax = np.abs(blocks).max(-1, keepdims=True)
    byte = np.maximum(np.where(amax > 0, np.frexp(amax)[1] - 1 + 127, 0) - down, 1)
    scale = np.exp2(byte - 127.0)
    codes = (blocks / scale).astype(np.float32).astype(dtype).astype(np.float64)
    return np.moveaxis((codes * scale).reshape(v.shape), -1, axis)


WIDE = False


def mx_kscale(k):
    if not WIDE:
        return np.ones(k)
    levels = np.array([18, -18])
    if k % 512:
        return np.exp2(np.random.permutation(np.resize(levels, k // 32))).repeat(32)
    a = np.empty((k // 512, 16))
    for p in range(k // 512):
        a[p, :8] = np.random.permutation(np.resize(levels, 8))
        for g in range(8):
            far = levels[np.abs(levels - a[p, g]) >= 10]
            a[p, g + 8] = far[np.random.randint(len(far))]
    return np.exp2(a.ravel()).repeat(32)


BF16 = ml_dtypes.bfloat16


def bf(x):
    return np.asarray(x, np.float32).astype(BF16)


def f64(x):
    return np.asarray(x).astype(np.float64)


BATCH, IN_F, OUT_F = 1024, 2048, 2048
Q_IN = IN_F // 4
Q_OUT = OUT_F // 4
MXB = 32


def setup_inputs():
    s = mx_kscale(BATCH)[:, None]
    uq = mx_kscale(OUT_F).reshape(Q_OUT // MXB, 4, MXB)[:, 0, :].reshape(Q_OUT)
    u = np.tile(uq, 4)
    c = 1.0 / np.sqrt(Q_IN)
    x = bf(np.random.standard_normal((BATCH, IN_F)) * s)
    Wr = bf(np.random.standard_normal((Q_OUT, Q_IN)) * c / uq[:, None])
    Wi = bf(np.random.standard_normal((Q_OUT, Q_IN)) * c / uq[:, None])
    Wj = bf(np.random.standard_normal((Q_OUT, Q_IN)) * c / uq[:, None])
    Wk = bf(np.random.standard_normal((Q_OUT, Q_IN)) * c / uq[:, None])
    b = bf(np.random.standard_normal(Q_OUT) * 0.5)
    g = bf(np.random.standard_normal((BATCH, OUT_F)) * np.exp2(np.random.randint(-6, 1, (BATCH, 1))) / s * u)
    return {"x": x, "Wr": Wr, "Wi": Wi, "Wj": Wj, "Wk": Wk, "b": b, "grad_out": g}


def reference(x, Wr, Wi, Wj, Wk, b, grad_out):
    g = f64(grad_out)

    gq = mxq(g, 1, "e5m2")
    g0 = gq[:, :Q_OUT]
    g1 = gq[:, Q_OUT:2 * Q_OUT]
    g2 = gq[:, 2 * Q_OUT:3 * Q_OUT]
    g3 = gq[:, 3 * Q_OUT:]
    r = mxq(f64(Wr), 0, "e4m3")
    i = mxq(f64(Wi), 0, "e4m3")
    j = mxq(f64(Wj), 0, "e4m3")
    k = mxq(f64(Wk), 0, "e4m3")
    dx0 = g0 @ r + g1 @ i + g2 @ j + g3 @ k
    dx1 = g1 @ r - g0 @ i + g3 @ j - g2 @ k
    dx2 = g2 @ r - g3 @ i - g0 @ j + g1 @ k
    dx3 = g3 @ r + g2 @ i - g1 @ j - g0 @ k
    dx = np.concatenate([dx0, dx1, dx2, dx3], axis=1)

    xt = mxq(f64(x), 0, "e4m3")
    gt = mxq(g, 0, "e5m2")
    dWr = (gt[:, :Q_OUT].T @ xt[:, :Q_IN]
        + gt[:, Q_OUT:2 * Q_OUT].T @ xt[:, Q_IN:2 * Q_IN]
        + gt[:, 2 * Q_OUT:3 * Q_OUT].T @ xt[:, 2 * Q_IN:3 * Q_IN]
        + gt[:, 3 * Q_OUT:].T @ xt[:, 3 * Q_IN:])
    return dx, dWr

@@ -1,0 +1,340 @@
+from contextlib import ExitStack
+
+import concourse.mybir as mybir
+from concourse.masks import make_identity
+
+P = 128
+PACK = 4
+BATCH, IN_F, OUT_F = 1024, 2048, 2048
+QW = 512
+K_PASS = P * PACK
+GROUPS = BATCH // K_PASS
+TILES = BATCH // P
+
+F32 = mybir.dt.float32
+BF16 = mybir.dt.bfloat16
+U32 = mybir.dt.uint32
+U8 = mybir.dt.uint8
+E4M3 = mybir.dt.float8_e4m3fn_x4
+E5M2 = mybir.dt.float8_e5m2_x4
+
+FLOPS = 2 * BATCH * OUT_F * IN_F + 2 * (4 * BATCH) * QW * QW
+BYTES = 2 * (BATCH * IN_F + BATCH * OUT_F + 4 * QW * QW) + 4 * (BATCH * IN_F + QW * QW)
+
+NEGATIVE = ((0, 1), (0, 2), (0, 3), (1, 3), (2, 1), (3, 2))
+OPERANDS = ((0, False), (1, False), (1, True), (2, False), (2, True), (3, False), (3, True))
+V_COLS = 384
+HEAD_GROUPS = ((0, 0), (0, 1), (0, 2), (0, 3), (1, 0), (1, 1))
+
+
+def tile_qdense_v_kernel(tc, x, Wr, Wi, Wj, Wk, b, grad_out, out_0, out_1):
+    nc = tc.nc
+    weights = (Wr, Wi, Wj, Wk)
+    g_rows = grad_out.rearrange("(g p j) w -> g p j w", g=GROUPS, j=PACK)
+    x_rows = x.rearrange("(g p j) w -> g p j w", g=GROUPS, j=PACK)
+    dx_rows = out_0.rearrange("(g p j) w -> g p j w", g=GROUPS, j=PACK)
+
+    with ExitStack() as ctx:
+        keep = ctx.enter_context(tc.tile_pool(name="keep", bufs=1))
+        work = ctx.enter_context(tc.tile_pool(name="work", bufs=3))
+        psum = ctx.enter_context(tc.psum_pool(name="psum", bufs=1))
+
+        ident = keep.tile([P, P], F32, name="ident")
+        make_identity(nc, ident[:])
+
+        g_raw = [keep.tile([P, PACK, OUT_F], BF16, name="g_raw%d" % i, align_bytes=64) for i in range(GROUPS)]
+        x_raw = [keep.tile([P, PACK, IN_F], BF16, name="x_raw%d" % i, align_bytes=64) for i in range(GROUPS)]
+        w_raw = [keep.tile([P, PACK, QW], BF16, name="w_raw%d" % i, align_bytes=64) for i in range(4)]
+        w_codes = {}
+        for op in OPERANDS:
+            w_codes[op] = (
+                keep.tile([P, QW], U32, name="wc%d%d" % (op[0], op[1]), align_bytes=64),
+                keep.tile([P, QW], U8, name="ws%d%d" % (op[0], op[1]), align_bytes=64),
+            )
+        blocks = []
+        for grp in range(GROUPS):
+            for src in ("g", "x"):
+                for q in range(4):
+                    blocks.append((src, grp, q))
+        t_codes = {}
+        for blk in blocks:
+            t_codes[blk] = (
+                keep.tile([P, QW], U32, name="tc%s%d%d" % blk, align_bytes=64),
+                keep.tile([P, QW], U8, name="ts%s%d%d" % blk, align_bytes=64),
+            )
+
+        ctx.enter_context(tc.manual_schedule())
+
+        def load_g(t, half=None):
+            grp, j = divmod(t, PACK)
+            cols = slice(0, OUT_F) if half is None else slice(1024 * half, 1024 * half + 1024)
+            nc.sync.dma_start(out=g_raw[grp][:, j, cols], in_=g_rows[grp, :, j, cols])
+
+        def load_w(w):
+            nc.sync.dma_start(out=w_raw[w][:], in_=weights[w].rearrange("(p j) w -> p j w", j=PACK))
+
+        def load_x(grp, half):
+            cols = slice(half * 1024, half * 1024 + 1024)
+            nc.sync.dma_start(out=x_raw[grp][:, :, cols], in_=x_rows[grp, :, :, cols])
+
+        w_grouped = {}
+        g_trans = {}
+        g_codes = {}
+        tr_banks = {}
+        acc = {}
+        out_tiles = {}
+        tok = {}
+        srt = {}
+
+        def sort(engine, t):
+            grp, j = divmod(t, PACK)
+            srt[t] = work.tile([P, 4, 2, P], F32, name="srt", tag="srt", bufs=2)
+            src = g_raw[grp][:, j, :].bitcast(F32).rearrange("p (q r u) -> p q u r", q=4, u=2)
+            if engine == "v":
+                nc.vector.tensor_copy(out=srt[t][:], in_=src)
+            else:
+                nc.scalar.copy(srt[t][:], src)
+
+        def transpose(t, h, bank_no):
+            grp, j = divmod(t, PACK)
+            words = g_raw[grp][:, j, :].bitcast(F32)
+            bank = psum.tile([P, 4, P], F32, name="bank%d" % bank_no, tag="bank%d" % bank_no)
+            tr_banks[t, h] = bank
+            for q in range(2):
+                for u in range(2):
+                    lo = 256 * (2 * h + q)
+                    if t in srt:
+                        src = srt[t][:, 2 * h + q, u, :]
+                    else:
+                        src = words[:, lo + u : lo + 256 : 2]
+                    nc.tensor.transpose(bank[:, 2 * q + u, :], src, ident[:])
+
+        def evac_transpose(t, h):
+            if h == 0:
+                g_trans[t] = work.tile([P, 4 * QW], BF16, name="g_trans", tag="g_trans", bufs=3, align_bytes=64)
+            dst = g_trans[t][:, 1024 * h : 1024 * h + 1024].bitcast(F32)
+            nc.scalar.copy(
+                dst.rearrange("p (q r u) -> p q r u", q=2, u=2),
+                tr_banks[t, h][:].rearrange("p (q u) r -> p q r u", q=2),
+            )
+
+        def quantize_g(t, parts=((0, 2),)):
+            if parts[0][0] == 0:
+                codes = work.tile([P, QW], U32, name="gc", tag="gc", bufs=4, align_bytes=64)
+                scales = work.tile([P, QW], U8, name="gs", tag="gs", bufs=4, align_bytes=64)
+                g_codes[t] = (codes, scales)
+            codes, scales = g_codes[t]
+            for lo, hi in parts:
+                nc.vector.quantize_mx(
+                    out=codes[:, 256 * lo : 256 * hi].bitcast(E5M2),
+                    scales=scales[:, 256 * lo : 256 * hi],
+                    in_=g_trans[t][:, 1024 * lo : 1024 * hi],
+                )
+
+        def interleave(engine, dst, src, lo, hi):
+            d = dst[:, lo:hi, :]
+            s = src.rearrange("p j c -> p c j")[:, lo:hi, :]
+            if engine == "v":
+                nc.vector.tensor_copy(out=d, in_=s)
+            else:
+                nc.scalar.copy(d, s)
+
+        def w_tile(w):
+            w_grouped[w, False] = work.tile([P, QW, PACK], BF16, name="w_grouped", tag="w_grouped", bufs=4, align_bytes=64)
+
+        def w_part(engine, w, lo, hi):
+            interleave(engine, w_grouped[w, False], w_raw[w][:], lo, hi)
+
+        def w_negate(w):
+            w_grouped[w, True] = work.tile([P, QW, PACK], BF16, name="w_negated", tag="w_negated", bufs=2, align_bytes=64)
+            nc.vector.tensor_scalar_mul(
+                w_grouped[w, True][:].rearrange("p c j -> p (c j)"),
+                w_grouped[w, False][:].rearrange("p c j -> p (c j)"),
+                -1.0,
+            )
+
+        def w_quantize(w, neg):
+            codes, scales = w_codes[w, neg]
+            nc.vector.quantize_mx(
+                out=codes[:].bitcast(E4M3),
+                scales=scales[:],
+                in_=w_grouped[w, neg][:].rearrange("p c j -> p (c j)"),
+            )
+
+        def open_acc(key, n):
+            acc[key] = psum.tile([P, QW], F32, name="bank%d" % n, tag="bank%d" % n)
+
+        def product(t, d, w):
+            q = d ^ w
+            wc, ws = w_codes[w, (q, d) in NEGATIVE]
+            gc, gs = g_codes[t]
+            cols = slice(q * P, q * P + P)
+            nc.tensor.matmul_mx(
+                out=acc[t, d][:],
+                lhsT=gc[:, cols].bitcast(E5M2),
+                lhsT_scale=gs[:, cols],
+                rhs=wc[:].bitcast(E4M3),
+                rhs_scale=ws[:],
+                start=(w == 0),
+                stop=(w == 3),
+            )
+
+        def evac(t, d):
+            grp, j = divmod(t, PACK)
+            h, e = divmod(d, 2)
+            if e == 0:
+                out_tiles[t, h] = work.tile([P, 2 * QW], F32, name="dx", tag="dx", bufs=5)
+            nc.scalar.copy(out_tiles[t, h][:, e * QW : e * QW + QW], acc[t, d][:])
+            if e == 1:
+                nc.sync.dma_start(out=dx_rows[grp, :, j, 1024 * h : 1024 * h + 1024], in_=out_tiles[t, h][:])
+
+        def tok_interleave(n):
+            src, grp, q = blocks[n]
+            raw = (g_raw if src == "g" else x_raw)[grp]
+            tok[n] = work.tile([P, QW, PACK], BF16, name="tok", tag="tok", bufs=4, align_bytes=64)
+            view = raw[:, :, q * QW : q * QW + QW]
+            interleave("v", tok[n], view, 0, V_COLS)
+            interleave("s", tok[n], view, V_COLS, QW)
+
+        def tok_quantize(n):
+            src = blocks[n][0]
+            codes, scales = t_codes[blocks[n]]
+            nc.vector.quantize_mx(
+                out=codes[:].bitcast(E5M2 if src == "g" else E4M3),
+                scales=scales[:],
+                in_=tok[n][:].rearrange("p c j -> p (c j)"),
+            )
+
+        units = []
+        for n in range(len(blocks) + 1):
+            if n < len(blocks):
+                units.append((tok_interleave, n))
+            if n >= 1:
+                units.append((tok_quantize, n - 1))
+        unit_pos = [0]
+
+        def run_units(upto):
+            while unit_pos[0] < min(upto, len(units)):
+                fn, n = units[unit_pos[0]]
+                fn(n)
+                unit_pos[0] += 1
+
+        load_w(0)
+        load_g(0, 0)
+        load_g(0, 1)
+        load_w(1)
+        load_g(1)
+        load_w(2)
+        load_g(2)
+        load_w(3)
+        load_g(3)
+        load_x(0, 0)
+        load_x(0, 1)
+        for w in range(4):
+            w_tile(w)
+        w_part("v", 0, 0, 384)
+        w_part("s", 0, 384, 512)
+        transpose(0, 0, 6)
+        evac_transpose(0, 0)
+        w_quantize(0, False)
+        transpose(0, 1, 7)
+        evac_transpose(0, 1)
+        quantize_g(0, ((0, 1),))
+        w_part("v", 1, 0, 256)
+        w_part("s", 1, 256, 512)
+        quantize_g(0, ((1, 2),))
+        for d in range(4):
+            open_acc((0, d), d)
+            product(0, d, 0)
+        transpose(1, 0, 6)
+        evac_transpose(1, 0)
+        transpose(1, 1, 7)
+        evac_transpose(1, 1)
+        w_quantize(1, False)
+        w_negate(1)
+        w_part("s", 2, 192, 512)
+        transpose(2, 0, 6)
+        transpose(2, 1, 7)
+        w_part("v", 2, 0, 192)
+        w_quantize(1, True)
+        quantize_g(1)
+        for d in range(2):
+            open_acc((1, d), 4 + d)
+            product(1, d, 0)
+        w_part("v", 3, 0, 192)
+        w_part("s", 3, 192, 512)
+        evac_transpose(2, 0)
+        evac_transpose(2, 1)
+        w_quantize(2, False)
+        w_negate(2)
+        w_quantize(3, False)
+        w_quantize(2, True)
+        w_negate(3)
+        quantize_g(2)
+        w_quantize(3, True)
+        for w, neg in OPERANDS[1:]:
+            for t, d in HEAD_GROUPS:
+                if ((d ^ w, d) in NEGATIVE) == neg:
+                    product(t, d, w)
+        load_g(4)
+        load_g(5)
+        pending = list(HEAD_GROUPS)
+
+        slots = [(1, 2), (1, 3)] + [(t, d) for t in range(2, TILES) for d in range(4)]
+        BANKS = (0, 1, 2, 3)
+        sorts = {0: (3,), 1: (4,), 5: (5,), 6: (6,), 14: (7,)}
+        runs = {2: (3, 4), 8: (5, 6), 16: (7,)}
+        quants = {5: (3,), 7: (4,), 11: (5,), 13: (6,), 19: (7,)}
+        loads = {1: ((load_g, (6,)),), 3: ((load_g, (7,)),), 5: ((load_x, (1, 0)),), 7: ((load_x, (1, 1)),)}
+        tr_queue = []
+        for s, (t, d) in enumerate(slots):
+            for fn, args in loads.get(s, ()):
+                fn(*args)
+            for nt in sorts.get(s, ()):
+                sort("v", nt)
+            for key in pending[:2]:
+                evac(key[0], key[1])
+            pending = pending[2:]
+            if tr_queue:
+                evac_transpose(*tr_queue.pop(0))
+            open_acc((t, d), BANKS[s % 4])
+            for w in range(4):
+                product(t, d, w)
+            pending.append((t, d))
+            for i, nt in enumerate(runs.get(s, ())):
+                for h in range(2):
+                    transpose(nt, h, 4 + 2 * i + h)
+                    tr_queue.append((nt, h))
+            for nt in quants.get(s, ()):
+                quantize_g(nt)
+            run_units(int(s * 1.1))
+
+        def dwr(m, grp):
+            for q in range(4):
+                gc, gs = t_codes["g", grp, q]
+                xc, xs = t_codes["x", grp, q]
+                cols = slice(m * P, m * P + P)
+                nc.tensor.matmul_mx(
+                    out=acc["m", m][:],
+                    lhsT=gc[:, cols].bitcast(E5M2),
+                    lhsT_scale=gs[:, cols],
+                    rhs=xc[:].bitcast(E4M3),
+                    rhs_scale=xs[:],
+                    start=(grp == 0 and q == 0),
+                    stop=(grp == GROUPS - 1 and q == 3),
+                )
+
+        for m in range(4):
+            for key in pending[:2]:
+                evac(key[0], key[1])
+            pending = pending[2:]
+            open_acc(("m", m), 4 + m)
+            dwr(m, 0)
+            run_units(int((len(slots) + m) * 1.1))
+        run_units(len(units))
+        for m in range(4):
+            dwr(m, 1)
+            res = work.tile([P, QW], F32, name="dw", tag="dx", bufs=5)
+            nc.scalar.copy(res[:, :256], acc["m", m][:, :256])
+            nc.vector.tensor_copy(out=res[:, 256:], in_=acc["m", m][:, 256:])
+            nc.sync.dma_start(out=out_1[m * P : m * P + P, :], in_=res[:])

@@ -132,8 +132,8 @@ def tile_qdense_v_kernel(tc, x, Wr, Wi, Wj, Wk, b, grad_out, out_0, out_1):
                 )
 
         def interleave(engine, dst, src, lo, hi):
-            d = dst[:, lo:hi, :]
-            s = src.rearrange("p j c -> p c j")[:, lo:hi, :]
+            d = dst[:, lo:hi, :].rearrange("p (c i) j -> p c j i", i=4)
+            s = src[:, :, lo:hi].rearrange("p j (c i) -> p c j i", i=4)
             if engine == "v":
                 nc.vector.tensor_copy(out=d, in_=s)
             else:
@@ -219,6 +219,14 @@ def tile_qdense_v_kernel(tc, x, Wr, Wi, Wj, Wk, b, grad_out, out_0, out_1):
                 fn(n)
                 unit_pos[0] += 1
 
+        zeros = keep.tile([P, QW], BF16, name="zeros")
+        nc.vector.memset(zeros[:], 0.0)
+
+        def warm(n, bank_no):
+            for i in range(n):
+                bank = psum.tile([P, QW], F32, name="bank%d" % bank_no, tag="bank%d" % bank_no)
+                nc.tensor.matmul(bank[:], lhsT=zeros[:, :P], rhs=zeros[:], start=True, stop=True)
+
         load_w(0)
         load_g(0, 0)
         load_g(0, 1)
@@ -232,12 +240,14 @@ def tile_qdense_v_kernel(tc, x, Wr, Wi, Wj, Wk, b, grad_out, out_0, out_1):
         load_x(0, 1)
         for w in range(4):
             w_tile(w)
-        w_part("v", 0, 0, 384)
-        w_part("s", 0, 384, 512)
+        w_part("v", 0, 0, 320)
+        w_part("s", 0, 320, 512)
+        warm(5, 0)
         transpose(0, 0, 6)
         evac_transpose(0, 0)
         w_quantize(0, False)
         transpose(0, 1, 7)
+        warm(2, 1)
         evac_transpose(0, 1)
         quantize_g(0, ((0, 1),))
         w_part("v", 1, 0, 256)
@@ -246,15 +256,15 @@ def tile_qdense_v_kernel(tc, x, Wr, Wi, Wj, Wk, b, grad_out, out_0, out_1):
         for d in range(4):
             open_acc((0, d), d)
             product(0, d, 0)
-        transpose(1, 0, 6)
+        transpose(1, 0, 4)
         evac_transpose(1, 0)
-        transpose(1, 1, 7)
+        transpose(1, 1, 5)
         evac_transpose(1, 1)
+        transpose(2, 0, 6)
+        transpose(2, 1, 7)
         w_quantize(1, False)
         w_negate(1)
         w_part("s", 2, 192, 512)
-        transpose(2, 0, 6)
-        transpose(2, 1, 7)
         w_part("v", 2, 0, 192)
         w_quantize(1, True)
         quantize_g(1)

@@ -24,7 +24,11 @@ BYTES = 2 * (BATCH * IN_F + BATCH * OUT_F + 4 * QW * QW) + 4 * (BATCH * IN_F + Q
 NEGATIVE = ((0, 1), (0, 2), (0, 3), (1, 3), (2, 1), (3, 2))
 OPERANDS = ((0, False), (1, False), (1, True), (2, False), (2, True), (3, False), (3, True))
 V_COLS = 384
-HEAD_GROUPS = ((0, 0), (0, 1), (0, 2), (0, 3), (1, 0), (1, 1))
+HEAD_GROUPS = ((0, 0), (0, 1), (0, 2), (0, 3), (1, 0), (1, 1), (1, 2), (1, 3))
+LAG = 1
+U0 = 2
+WS = (320, 256, 256, 320)
+U1 = 1.2
 
 
 def tile_qdense_v_kernel(tc, x, Wr, Wi, Wj, Wk, b, grad_out, out_0, out_1):
@@ -109,14 +113,16 @@ def tile_qdense_v_kernel(tc, x, Wr, Wi, Wj, Wk, b, grad_out, out_0, out_1):
                         src = words[:, lo + u : lo + 256 : 2]
                     nc.tensor.transpose(bank[:, 2 * q + u, :], src, ident[:])
 
-        def evac_transpose(t, h):
+        def evac_transpose(t, h, engine="s"):
             if h == 0:
                 g_trans[t] = work.tile([P, 4 * QW], BF16, name="g_trans", tag="g_trans", bufs=3, align_bytes=64)
             dst = g_trans[t][:, 1024 * h : 1024 * h + 1024].bitcast(F32)
-            nc.scalar.copy(
-                dst.rearrange("p (q r u) -> p q r u", q=2, u=2),
-                tr_banks[t, h][:].rearrange("p (q u) r -> p q r u", q=2),
-            )
+            dst = dst.rearrange("p (q r u) -> p q r u", q=2, u=2)
+            src = tr_banks[t, h][:].rearrange("p (q u) r -> p q r u", q=2)
+            if engine == "v":
+                nc.vector.tensor_copy(out=dst, in_=src)
+            else:
+                nc.scalar.copy(dst, src)
 
         def quantize_g(t, parts=((0, 2),)):
             if parts[0][0] == 0:
@@ -179,12 +185,16 @@ def tile_qdense_v_kernel(tc, x, Wr, Wi, Wj, Wk, b, grad_out, out_0, out_1):
                 stop=(w == 3),
             )
 
-        def evac(t, d):
+        def evac(t, d, engine="s"):
             grp, j = divmod(t, PACK)
             h, e = divmod(d, 2)
             if e == 0:
                 out_tiles[t, h] = work.tile([P, 2 * QW], F32, name="dx", tag="dx", bufs=5)
-            nc.scalar.copy(out_tiles[t, h][:, e * QW : e * QW + QW], acc[t, d][:])
+            dst = out_tiles[t, h][:, e * QW : e * QW + QW]
+            if engine == "v":
+                nc.vector.tensor_copy(out=dst, in_=acc[t, d][:])
+            else:
+                nc.scalar.copy(dst, acc[t, d][:])
             if e == 1:
                 nc.sync.dma_start(out=dx_rows[grp, :, j, 1024 * h : 1024 * h + 1024], in_=out_tiles[t, h][:])
 
@@ -236,12 +246,12 @@ def tile_qdense_v_kernel(tc, x, Wr, Wi, Wj, Wk, b, grad_out, out_0, out_1):
         load_g(2)
         load_w(3)
         load_g(3)
-        load_x(0, 0)
-        load_x(0, 1)
+        load_g(4)
+        load_g(5)
         for w in range(4):
             w_tile(w)
-        w_part("v", 0, 0, 320)
-        w_part("s", 0, 320, 512)
+        w_part("v", 0, 0, WS[0])
+        w_part("s", 0, WS[0], 512)
         warm(5, 0)
         transpose(0, 0, 6)
         evac_transpose(0, 0)
@@ -250,8 +260,8 @@ def tile_qdense_v_kernel(tc, x, Wr, Wi, Wj, Wk, b, grad_out, out_0, out_1):
         warm(2, 1)
         evac_transpose(0, 1)
         quantize_g(0, ((0, 1),))
-        w_part("v", 1, 0, 256)
-        w_part("s", 1, 256, 512)
+        w_part("v", 1, 0, WS[1])
+        w_part("s", 1, WS[1], 512)
         quantize_g(0, ((1, 2),))
         for d in range(4):
             open_acc((0, d), d)
@@ -264,49 +274,55 @@ def tile_qdense_v_kernel(tc, x, Wr, Wi, Wj, Wk, b, grad_out, out_0, out_1):
         transpose(2, 1, 7)
         w_quantize(1, False)
         w_negate(1)
-        w_part("s", 2, 192, 512)
-        w_part("v", 2, 0, 192)
+        w_part("s", 2, WS[2], 512)
+        w_part("v", 2, 0, WS[2])
         w_quantize(1, True)
         quantize_g(1)
-        for d in range(2):
-            open_acc((1, d), 4 + d)
-            product(1, d, 0)
-        w_part("v", 3, 0, 192)
-        w_part("s", 3, 192, 512)
+        w_part("v", 3, 0, WS[3])
         evac_transpose(2, 0)
         evac_transpose(2, 1)
+        w_part("s", 3, WS[3], 512)
         w_quantize(2, False)
         w_negate(2)
         w_quantize(3, False)
         w_quantize(2, True)
         w_negate(3)
-        quantize_g(2)
         w_quantize(3, True)
-        for w, neg in OPERANDS[1:]:
+        quantize_g(2)
+        for n in range(1, len(OPERANDS) + LAG):
             for t, d in HEAD_GROUPS:
+                if n - LAG * t < 0 or n - LAG * t >= len(OPERANDS):
+                    continue
+                w, neg = OPERANDS[n - LAG * t]
                 if ((d ^ w, d) in NEGATIVE) == neg:
+                    if w == 0:
+                        open_acc((t, d), 4 + d)
                     product(t, d, w)
-        load_g(4)
-        load_g(5)
+        load_g(6)
+        load_x(0, 0)
         pending = list(HEAD_GROUPS)
 
-        slots = [(1, 2), (1, 3)] + [(t, d) for t in range(2, TILES) for d in range(4)]
+        slots = [(t, d) for t in range(2, TILES) for d in range(4)]
         BANKS = (0, 1, 2, 3)
-        sorts = {0: (3,), 1: (4,), 5: (5,), 6: (6,), 14: (7,)}
-        runs = {2: (3, 4), 8: (5, 6), 16: (7,)}
-        quants = {5: (3,), 7: (4,), 11: (5,), 13: (6,), 19: (7,)}
-        loads = {1: ((load_g, (6,)),), 3: ((load_g, (7,)),), 5: ((load_x, (1, 0)),), 7: ((load_x, (1, 1)),)}
+        sorts = {4: (5,), 5: (6,), 12: (7,)}
+        runs = {2: (3, 4), 6: (5, 6), 14: (7,)}
+        quants = {3: (3,), 5: (4,), 9: (5,), 11: (6,), 17: (7,)}
+        TRN = {3: 2}
+        loads = {1: ((load_x, (0, 1)),), 5: ((load_g, (7,)),), 7: ((load_x, (1, 0)),), 9: ((load_x, (1, 1)),)}
         tr_queue = []
+        sort("v", 3)
+        sort("v", 4)
         for s, (t, d) in enumerate(slots):
             for fn, args in loads.get(s, ()):
                 fn(*args)
             for nt in sorts.get(s, ()):
                 sort("v", nt)
-            for key in pending[:2]:
-                evac(key[0], key[1])
-            pending = pending[2:]
-            if tr_queue:
-                evac_transpose(*tr_queue.pop(0))
+            for i, key in enumerate(pending[:3]):
+                evac(key[0], key[1], "svs"[i])
+            pending = pending[3:]
+            for i in range(TRN.get(s, 1)):
+                if tr_queue:
+                    evac_transpose(*tr_queue.pop(0), "sv"[i])
             open_acc((t, d), BANKS[s % 4])
             for w in range(4):
                 product(t, d, w)
@@ -317,7 +333,7 @@ def tile_qdense_v_kernel(tc, x, Wr, Wi, Wj, Wk, b, grad_out, out_0, out_1):
                     tr_queue.append((nt, h))
             for nt in quants.get(s, ()):
                 quantize_g(nt)
-            run_units(int(s * 1.1))
+            run_units(int(max(0, s - U0) * U1))
 
         def dwr(m, grp):
             for q in range(4):
@@ -335,12 +351,12 @@ def tile_qdense_v_kernel(tc, x, Wr, Wi, Wj, Wk, b, grad_out, out_0, out_1):
                 )
 
         for m in range(4):
-            for key in pending[:2]:
+            for key in pending:
                 evac(key[0], key[1])
-            pending = pending[2:]
+            pending = []
             open_acc(("m", m), 4 + m)
             dwr(m, 0)
-            run_units(int((len(slots) + m) * 1.1))
+            run_units(int((len(slots) + m + 1 - U0) * U1))
         run_units(len(units))
         for m in range(4):
             dwr(m, 1)

@@ -25,10 +25,10 @@ NEGATIVE = ((0, 1), (0, 2), (0, 3), (1, 3), (2, 1), (3, 2))
 OPERANDS = ((0, False), (1, False), (1, True), (2, False), (2, True), (3, False), (3, True))
 V_COLS = 384
 HEAD_GROUPS = ((0, 0), (0, 1), (0, 2), (0, 3), (1, 0), (1, 1), (1, 2), (1, 3))
-LAG = 1
-U0 = 2
-WS = (320, 256, 256, 320)
-U1 = 1.2
+LAG = 2
+U0 = 0
+WS = (320, 256, 320, 320)
+U1 = 1.4
 
 
 def tile_qdense_v_kernel(tc, x, Wr, Wi, Wj, Wk, b, grad_out, out_0, out_1):
@@ -237,6 +237,14 @@ def tile_qdense_v_kernel(tc, x, Wr, Wi, Wj, Wk, b, grad_out, out_0, out_1):
                 bank = psum.tile([P, QW], F32, name="bank%d" % bank_no, tag="bank%d" % bank_no)
                 nc.tensor.matmul(bank[:], lhsT=zeros[:, :P], rhs=zeros[:], start=True, stop=True)
 
+        def head_products(t, n):
+            w, neg = OPERANDS[n]
+            for d in range(4):
+                if ((d ^ w, d) in NEGATIVE) == neg:
+                    if w == 0:
+                        open_acc((t, d), 4 * t + d)
+                    product(t, d, w)
+
         load_w(0)
         load_g(0, 0)
         load_g(0, 1)
@@ -263,16 +271,15 @@ def tile_qdense_v_kernel(tc, x, Wr, Wi, Wj, Wk, b, grad_out, out_0, out_1):
         w_part("v", 1, 0, WS[1])
         w_part("s", 1, WS[1], 512)
         quantize_g(0, ((1, 2),))
-        for d in range(4):
-            open_acc((0, d), d)
-            product(0, d, 0)
+        head_products(0, 0)
         transpose(1, 0, 4)
         evac_transpose(1, 0)
         transpose(1, 1, 5)
         evac_transpose(1, 1)
+        w_quantize(1, False)
+        head_products(0, 1)
         transpose(2, 0, 6)
         transpose(2, 1, 7)
-        w_quantize(1, False)
         w_negate(1)
         w_part("s", 2, WS[2], 512)
         w_part("v", 2, 0, WS[2])
@@ -289,15 +296,10 @@ def tile_qdense_v_kernel(tc, x, Wr, Wi, Wj, Wk, b, grad_out, out_0, out_1):
         w_negate(3)
         w_quantize(3, True)
         quantize_g(2)
-        for n in range(1, len(OPERANDS) + LAG):
-            for t, d in HEAD_GROUPS:
-                if n - LAG * t < 0 or n - LAG * t >= len(OPERANDS):
-                    continue
-                w, neg = OPERANDS[n - LAG * t]
-                if ((d ^ w, d) in NEGATIVE) == neg:
-                    if w == 0:
-                        open_acc((t, d), 4 + d)
-                    product(t, d, w)
+        for n in range(2, len(OPERANDS) + LAG):
+            for t in range(2):
+                if 0 <= n - LAG * t < len(OPERANDS):
+                    head_products(t, n - LAG * t)
         load_g(6)
         load_x(0, 0)
         pending = list(HEAD_GROUPS)

@@ -23,12 +23,12 @@ BYTES = 2 * (BATCH * IN_F + BATCH * OUT_F + 4 * QW * QW) + 4 * (BATCH * IN_F + Q
 
 NEGATIVE = ((0, 1), (0, 2), (0, 3), (1, 3), (2, 1), (3, 2))
 OPERANDS = ((0, False), (1, False), (1, True), (2, False), (2, True), (3, False), (3, True))
-V_COLS = 384
+V_COLS = 416
 HEAD_GROUPS = ((0, 0), (0, 1), (0, 2), (0, 3), (1, 0), (1, 1), (1, 2), (1, 3))
 LAG = 2
 U0 = 0
 WS = (320, 256, 320, 320)
-U1 = 1.4
+U1 = 1.25
 
 
 def tile_qdense_v_kernel(tc, x, Wr, Wi, Wj, Wk, b, grad_out, out_0, out_1):
@@ -170,7 +170,7 @@ def tile_qdense_v_kernel(tc, x, Wr, Wi, Wj, Wk, b, grad_out, out_0, out_1):
         def open_acc(key, n):
             acc[key] = psum.tile([P, QW], F32, name="bank%d" % n, tag="bank%d" % n)
 
-        def product(t, d, w):
+        def product(t, d, w, first, last):
             q = d ^ w
             wc, ws = w_codes[w, (q, d) in NEGATIVE]
             gc, gs = g_codes[t]
@@ -181,8 +181,8 @@ def tile_qdense_v_kernel(tc, x, Wr, Wi, Wj, Wk, b, grad_out, out_0, out_1):
                 lhsT_scale=gs[:, cols],
                 rhs=wc[:].bitcast(E4M3),
                 rhs_scale=ws[:],
-                start=(w == 0),
-                stop=(w == 3),
+                start=first,
+                stop=last,
             )
 
         def evac(t, d, engine="s"):
@@ -243,7 +243,7 @@ def tile_qdense_v_kernel(tc, x, Wr, Wi, Wj, Wk, b, grad_out, out_0, out_1):
                 if ((d ^ w, d) in NEGATIVE) == neg:
                     if w == 0:
                         open_acc((t, d), 4 * t + d)
-                    product(t, d, w)
+                    product(t, d, w, w == 0, w == 3)
 
         load_w(0)
         load_g(0, 0)
@@ -302,10 +302,9 @@ def tile_qdense_v_kernel(tc, x, Wr, Wi, Wj, Wk, b, grad_out, out_0, out_1):
                     head_products(t, n - LAG * t)
         load_g(6)
         load_x(0, 0)
-        pending = list(HEAD_GROUPS)
-
         slots = [(t, d) for t in range(2, TILES) for d in range(4)]
         BANKS = (0, 1, 2, 3)
+        QORD = ((0, 1, 2, 3), (0, 1, 2, 3))
         sorts = {4: (5,), 5: (6,), 12: (7,)}
         runs = {2: (3, 4), 6: (5, 6), 14: (7,)}
         quants = {3: (3,), 5: (4,), 9: (5,), 11: (6,), 17: (7,)}
@@ -314,25 +313,31 @@ def tile_qdense_v_kernel(tc, x, Wr, Wi, Wj, Wk, b, grad_out, out_0, out_1):
         tr_queue = []
         sort("v", 3)
         sort("v", 4)
+        finished = list(HEAD_GROUPS)
         for s, (t, d) in enumerate(slots):
             for fn, args in loads.get(s, ()):
                 fn(*args)
             for nt in sorts.get(s, ()):
                 sort("v", nt)
-            for i, key in enumerate(pending[:3]):
+            take = 3 if len(finished) > 2 else 1
+            for i, key in enumerate(finished[:take]):
                 evac(key[0], key[1], "svs"[i])
-            pending = pending[3:]
+            finished = finished[take:]
             for i in range(TRN.get(s, 1)):
                 if tr_queue:
                     evac_transpose(*tr_queue.pop(0), "sv"[i])
-            open_acc((t, d), BANKS[s % 4])
-            for w in range(4):
-                product(t, d, w)
-            pending.append((t, d))
             for i, nt in enumerate(runs.get(s, ())):
                 for h in range(2):
                     transpose(nt, h, 4 + 2 * i + h)
                     tr_queue.append((nt, h))
+            if d % 2 == 0:
+                for e in (d, d + 1):
+                    open_acc((t, e), BANKS[(s + e - d) % 4])
+                for i, q in enumerate(QORD[d // 2]):
+                    for e in (d, d + 1):
+                        product(t, e, q ^ e, i == 0, i == 3)
+            else:
+                finished += [(t, d - 1), (t, d)]
             for nt in quants.get(s, ()):
                 quantize_g(nt)
             run_units(int(max(0, s - U0) * U1))
@@ -353,9 +358,9 @@ def tile_qdense_v_kernel(tc, x, Wr, Wi, Wj, Wk, b, grad_out, out_0, out_1):
                 )
 
         for m in range(4):
-            for key in pending:
+            for key in finished[:1]:
                 evac(key[0], key[1])
-            pending = []
+            finished = finished[1:]
             open_acc(("m", m), 4 + m)
             dwr(m, 0)
             run_units(int((len(slots) + m + 1 - U0) * U1))

from contextlib import ExitStack

import concourse.mybir as mybir
from concourse.masks import make_identity

P = 128
PACK = 4
BATCH, IN_F, OUT_F = 1024, 2048, 2048
QW = 512
K_PASS = P * PACK
GROUPS = BATCH // K_PASS
TILES = BATCH // P

F32 = mybir.dt.float32
BF16 = mybir.dt.bfloat16
U32 = mybir.dt.uint32
U8 = mybir.dt.uint8
E4M3 = mybir.dt.float8_e4m3fn_x4
E5M2 = mybir.dt.float8_e5m2_x4

FLOPS = 2 * BATCH * OUT_F * IN_F + 2 * (4 * BATCH) * QW * QW
BYTES = 2 * (BATCH * IN_F + BATCH * OUT_F + 4 * QW * QW) + 4 * (BATCH * IN_F + QW * QW)

NEGATIVE = ((0, 1), (0, 2), (0, 3), (1, 3), (2, 1), (3, 2))
OPERANDS = ((0, False), (1, False), (1, True), (2, False), (2, True), (3, False), (3, True))
V_COLS = 416
HEAD_GROUPS = ((0, 0), (0, 1), (0, 2), (0, 3), (1, 0), (1, 1), (1, 2), (1, 3))
LAG = 2
U0 = 0
WS = (320, 256, 320, 320)
U1 = 1.25


def tile_qdense_v_kernel(tc, x, Wr, Wi, Wj, Wk, b, grad_out, out_0, out_1):
    nc = tc.nc
    weights = (Wr, Wi, Wj, Wk)
    g_rows = grad_out.rearrange("(g p j) w -> g p j w", g=GROUPS, j=PACK)
    x_rows = x.rearrange("(g p j) w -> g p j w", g=GROUPS, j=PACK)
    dx_rows = out_0.rearrange("(g p j) w -> g p j w", g=GROUPS, j=PACK)

    with ExitStack() as ctx:
        keep = ctx.enter_context(tc.tile_pool(name="keep", bufs=1))
        work = ctx.enter_context(tc.tile_pool(name="work", bufs=3))
        psum = ctx.enter_context(tc.psum_pool(name="psum", bufs=1))

        ident = keep.tile([P, P], F32, name="ident")
        make_identity(nc, ident[:])

        g_raw = [keep.tile([P, PACK, OUT_F], BF16, name="g_raw%d" % i, align_bytes=64) for i in range(GROUPS)]
        x_raw = [keep.tile([P, PACK, IN_F], BF16, name="x_raw%d" % i, align_bytes=64) for i in range(GROUPS)]
        w_raw = [keep.tile([P, PACK, QW], BF16, name="w_raw%d" % i, align_bytes=64) for i in range(4)]
        w_codes = {}
        for op in OPERANDS:
            w_codes[op] = (
                keep.tile([P, QW], U32, name="wc%d%d" % (op[0], op[1]), align_bytes=64),
                keep.tile([P, QW], U8, name="ws%d%d" % (op[0], op[1]), align_bytes=64),
            )
        blocks = []
        for grp in range(GROUPS):
            for src in ("g", "x"):
                for q in range(4):
                    blocks.append((src, grp, q))
        t_codes = {}
        for blk in blocks:
            t_codes[blk] = (
                keep.tile([P, QW], U32, name="tc%s%d%d" % blk, align_bytes=64),
                keep.tile([P, QW], U8, name="ts%s%d%d" % blk, align_bytes=64),
            )

        ctx.enter_context(tc.manual_schedule())

        def load_g(t, half=None):
            grp, j = divmod(t, PACK)
            cols = slice(0, OUT_F) if half is None else slice(1024 * half, 1024 * half + 1024)
            nc.sync.dma_start(out=g_raw[grp][:, j, cols], in_=g_rows[grp, :, j, cols])

        def load_w(w):
            nc.sync.dma_start(out=w_raw[w][:], in_=weights[w].rearrange("(p j) w -> p j w", j=PACK))

        def load_x(grp, half):
            cols = slice(half * 1024, half * 1024 + 1024)
            nc.sync.dma_start(out=x_raw[grp][:, :, cols], in_=x_rows[grp, :, :, cols])

        w_grouped = {}
        g_trans = {}
        g_codes = {}
        tr_banks = {}
        acc = {}
        out_tiles = {}
        tok = {}
        srt = {}

        def sort(engine, t):
            grp, j = divmod(t, PACK)
            srt[t] = work.tile([P, 4, 2, P], F32, name="srt", tag="srt", bufs=2)
            src = g_raw[grp][:, j, :].bitcast(F32).rearrange("p (q r u) -> p q u r", q=4, u=2)
            if engine == "v":
                nc.vector.tensor_copy(out=srt[t][:], in_=src)
            else:
                nc.scalar.copy(srt[t][:], src)

        def transpose(t, h, bank_no):
            grp, j = divmod(t, PACK)
            words = g_raw[grp][:, j, :].bitcast(F32)
            bank = psum.tile([P, 4, P], F32, name="bank%d" % bank_no, tag="bank%d" % bank_no)
            tr_banks[t, h] = bank
            for q in range(2):
                for u in range(2):
                    lo = 256 * (2 * h + q)
                    if t in srt:
                        src = srt[t][:, 2 * h + q, u, :]
                    else:
                        src = words[:, lo + u : lo + 256 : 2]
                    nc.tensor.transpose(bank[:, 2 * q + u, :], src, ident[:])

        def evac_transpose(t, h, engine="s"):
            if h == 0:
                g_trans[t] = work.tile([P, 4 * QW], BF16, name="g_trans", tag="g_trans", bufs=3, align_bytes=64)
            dst = g_trans[t][:, 1024 * h : 1024 * h + 1024].bitcast(F32)
            dst = dst.rearrange("p (q r u) -> p q r u", q=2, u=2)
            src = tr_banks[t, h][:].rearrange("p (q u) r -> p q r u", q=2)
            if engine == "v":
                nc.vector.tensor_copy(out=dst, in_=src)
            else:
                nc.scalar.copy(dst, src)

        def quantize_g(t, parts=((0, 2),)):
            if parts[0][0] == 0:
                codes = work.tile([P, QW], U32, name="gc", tag="gc", bufs=4, align_bytes=64)
                scales = work.tile([P, QW], U8, name="gs", tag="gs", bufs=4, align_bytes=64)
                g_codes[t] = (codes, scales)
            codes, scales = g_codes[t]
            for lo, hi in parts:
                nc.vector.quantize_mx(
                    out=codes[:, 256 * lo : 256 * hi].bitcast(E5M2),
                    scales=scales[:, 256 * lo : 256 * hi],
                    in_=g_trans[t][:, 1024 * lo : 1024 * hi],
                )

        def interleave(engine, dst, src, lo, hi):
            d = dst[:, lo:hi, :].rearrange("p (c i) j -> p c j i", i=4)
            s = src[:, :, lo:hi].rearrange("p j (c i) -> p c j i", i=4)
            if engine == "v":
                nc.vector.tensor_copy(out=d, in_=s)
            else:
                nc.scalar.copy(d, s)

        def w_tile(w):
            w_grouped[w, False] = work.tile([P, QW, PACK], BF16, name="w_grouped", tag="w_grouped", bufs=4, align_bytes=64)

        def w_part(engine, w, lo, hi):
            interleave(engine, w_grouped[w, False], w_raw[w][:], lo, hi)

        def w_negate(w):
            w_grouped[w, True] = work.tile([P, QW, PACK], BF16, name="w_negated", tag="w_negated", bufs=2, align_bytes=64)
            nc.vector.tensor_scalar_mul(
                w_grouped[w, True][:].rearrange("p c j -> p (c j)"),
                w_grouped[w, False][:].rearrange("p c j -> p (c j)"),
                -1.0,
            )

        def w_quantize(w, neg):
            codes, scales = w_codes[w, neg]
            nc.vector.quantize_mx(
                out=codes[:].bitcast(E4M3),
                scales=scales[:],
                in_=w_grouped[w, neg][:].rearrange("p c j -> p (c j)"),
            )

        def open_acc(key, n):
            acc[key] = psum.tile([P, QW], F32, name="bank%d" % n, tag="bank%d" % n)

        def product(t, d, w, first, last):
            q = d ^ w
            wc, ws = w_codes[w, (q, d) in NEGATIVE]
            gc, gs = g_codes[t]
            cols = slice(q * P, q * P + P)
            nc.tensor.matmul_mx(
                out=acc[t, d][:],
                lhsT=gc[:, cols].bitcast(E5M2),
                lhsT_scale=gs[:, cols],
                rhs=wc[:].bitcast(E4M3),
                rhs_scale=ws[:],
                start=first,
                stop=last,
            )

        def evac(t, d, engine="s"):
            grp, j = divmod(t, PACK)
            h, e = divmod(d, 2)
            if e == 0:
                out_tiles[t, h] = work.tile([P, 2 * QW], F32, name="dx", tag="dx", bufs=5)
            dst = out_tiles[t, h][:, e * QW : e * QW + QW]
            if engine == "v":
                nc.vector.tensor_copy(out=dst, in_=acc[t, d][:])
            else:
                nc.scalar.copy(dst, acc[t, d][:])
            if e == 1:
                nc.sync.dma_start(out=dx_rows[grp, :, j, 1024 * h : 1024 * h + 1024], in_=out_tiles[t, h][:])

        def tok_interleave(n):
            src, grp, q = blocks[n]
            raw = (g_raw if src == "g" else x_raw)[grp]
            tok[n] = work.tile([P, QW, PACK], BF16, name="tok", tag="tok", bufs=4, align_bytes=64)
            view = raw[:, :, q * QW : q * QW + QW]
            interleave("v", tok[n], view, 0, V_COLS)
            interleave("s", tok[n], view, V_COLS, QW)

        def tok_quantize(n):
            src = blocks[n][0]
            codes, scales = t_codes[blocks[n]]
            nc.vector.quantize_mx(
                out=codes[:].bitcast(E5M2 if src == "g" else E4M3),
                scales=scales[:],
                in_=tok[n][:].rearrange("p c j -> p (c j)"),
            )

        units = []
        for n in range(len(blocks) + 1):
            if n < len(blocks):
                units.append((tok_interleave, n))
            if n >= 1:
                units.append((tok_quantize, n - 1))
        unit_pos = [0]

        def run_units(upto):
            while unit_pos[0] < min(upto, len(units)):
                fn, n = units[unit_pos[0]]
                fn(n)
                unit_pos[0] += 1

        zeros = keep.tile([P, QW], BF16, name="zeros")
        nc.vector.memset(zeros[:], 0.0)

        def warm(n, bank_no):
            for i in range(n):
                bank = psum.tile([P, QW], F32, name="bank%d" % bank_no, tag="bank%d" % bank_no)
                nc.tensor.matmul(bank[:], lhsT=zeros[:, :P], rhs=zeros[:], start=True, stop=True)

        def head_products(t, n):
            w, neg = OPERANDS[n]
            for d in range(4):
                if ((d ^ w, d) in NEGATIVE) == neg:
                    if w == 0:
                        open_acc((t, d), 4 * t + d)
                    product(t, d, w, w == 0, w == 3)

        load_w(0)
        load_g(0, 0)
        load_g(0, 1)
        load_w(1)
        load_g(1)
        load_w(2)
        load_g(2)
        load_w(3)
        load_g(3)
        load_g(4)
        load_g(5)
        for w in range(4):
            w_tile(w)
        w_part("v", 0, 0, WS[0])
        w_part("s", 0, WS[0], 512)
        warm(5, 0)
        transpose(0, 0, 6)
        evac_transpose(0, 0)
        w_quantize(0, False)
        transpose(0, 1, 7)
        warm(2, 1)
        evac_transpose(0, 1)
        quantize_g(0, ((0, 1),))
        w_part("v", 1, 0, WS[1])
        w_part("s", 1, WS[1], 512)
        quantize_g(0, ((1, 2),))
        head_products(0, 0)
        transpose(1, 0, 4)
        evac_transpose(1, 0)
        transpose(1, 1, 5)
        evac_transpose(1, 1)
        w_quantize(1, False)
        head_products(0, 1)
        transpose(2, 0, 6)
        transpose(2, 1, 7)
        w_negate(1)
        w_part("s", 2, WS[2], 512)
        w_part("v", 2, 0, WS[2])
        w_quantize(1, True)
        quantize_g(1)
        w_part("v", 3, 0, WS[3])
        evac_transpose(2, 0)
        evac_transpose(2, 1)
        w_part("s", 3, WS[3], 512)
        w_quantize(2, False)
        w_negate(2)
        w_quantize(3, False)
        w_quantize(2, True)
        w_negate(3)
        w_quantize(3, True)
        quantize_g(2)
        for n in range(2, len(OPERANDS) + LAG):
            for t in range(2):
                if 0 <= n - LAG * t < len(OPERANDS):
                    head_products(t, n - LAG * t)
        load_g(6)
        load_x(0, 0)
        slots = [(t, d) for t in range(2, TILES) for d in range(4)]
        BANKS = (0, 1, 2, 3)
        QORD = ((0, 1, 2, 3), (0, 1, 2, 3))
        sorts = {4: (5,), 5: (6,), 12: (7,)}
        runs = {2: (3, 4), 6: (5, 6), 14: (7,)}
        quants = {3: (3,), 5: (4,), 9: (5,), 11: (6,), 17: (7,)}
        TRN = {3: 2}
        loads = {1: ((load_x, (0, 1)),), 5: ((load_g, (7,)),), 7: ((load_x, (1, 0)),), 9: ((load_x, (1, 1)),)}
        tr_queue = []
        sort("v", 3)
        sort("v", 4)
        finished = list(HEAD_GROUPS)
        for s, (t, d) in enumerate(slots):
            for fn, args in loads.get(s, ()):
                fn(*args)
            for nt in sorts.get(s, ()):
                sort("v", nt)
            take = 3 if len(finished) > 2 else 1
            for i, key in enumerate(finished[:take]):
                evac(key[0], key[1], "svs"[i])
            finished = finished[take:]
            for i in range(TRN.get(s, 1)):
                if tr_queue:
                    evac_transpose(*tr_queue.pop(0), "sv"[i])
            for i, nt in enumerate(runs.get(s, ())):
                for h in range(2):
                    transpose(nt, h, 4 + 2 * i + h)
                    tr_queue.append((nt, h))
            if d % 2 == 0:
                for e in (d, d + 1):
                    open_acc((t, e), BANKS[(s + e - d) % 4])
                for i, q in enumerate(QORD[d // 2]):
                    for e in (d, d + 1):
                        product(t, e, q ^ e, i == 0, i == 3)
            else:
                finished += [(t, d - 1), (t, d)]
            for nt in quants.get(s, ()):
                quantize_g(nt)
            run_units(int(max(0, s - U0) * U1))

        def dwr(m, grp):
            for q in range(4):
                gc, gs = t_codes["g", grp, q]
                xc, xs = t_codes["x", grp, q]
                cols = slice(m * P, m * P + P)
                nc.tensor.matmul_mx(
                    out=acc["m", m][:],
                    lhsT=gc[:, cols].bitcast(E5M2),
                    lhsT_scale=gs[:, cols],
                    rhs=xc[:].bitcast(E4M3),
                    rhs_scale=xs[:],
                    start=(grp == 0 and q == 0),
                    stop=(grp == GROUPS - 1 and q == 3),
                )

        for m in range(4):
            for key in finished[:1]:
                evac(key[0], key[1])
            finished = finished[1:]
            open_acc(("m", m), 4 + m)
            dwr(m, 0)
            run_units(int((len(slots) + m + 1 - U0) * U1))
        run_units(len(units))
        for m in range(4):
            dwr(m, 1)
            res = work.tile([P, QW], F32, name="dw", tag="dx", bufs=5)
            nc.scalar.copy(res[:, :256], acc["m", m][:, :256])
            nc.vector.tensor_copy(out=res[:, 256:], in_=acc["m", m][:, 256:])
            nc.sync.dma_start(out=out_1[m * P : m * P + P, :], in_=res[:])
